import numpy as np
import ml_dtypes

BF16 = ml_dtypes.bfloat16


def bf(x):
    return np.asarray(x, np.float32).astype(BF16)


def f32(x):
    return np.asarray(x, np.float32)


def f64(x):
    return np.asarray(x).astype(np.float64)


def striped(idx):
    return np.tile(idx.reshape(-1, 16).T, (8, 1))


C, S, N, H, E = 128, 512, 128, 256, 128
R = np.sqrt(0.5)


def setup_inputs():
    return {"x": f32(np.random.standard_normal((C, S))), "dst": f32(np.random.standard_normal((C, N))), "w": bf(np.random.standard_normal((C, H)) / np.sqrt(C)), "b": f32(0.1 * np.random.standard_normal((H, 1))), "w_mu": bf(np.random.standard_normal((H, E)) * np.sqrt(2.0 / H)), "b_mu": f32(0.1 * np.random.standard_normal((E, 1))), "offs": striped(np.random.permutation(np.tile(np.arange(S), 2))[:N])}


def reference(x, dst, w, b, w_mu, b_mu, offs):
    idx = offs[:16].T.reshape(-1)
    agg = R * (f64(x)[:, idx] + R * f64(dst))
    rep = np.maximum(f64(w).T @ agg + f64(b), 0.0)
    return np.maximum(f64(w_mu).T @ rep + f64(b_mu), 0.0)

@@ -1,0 +1,59 @@
+import math
+
+import concourse.mybir as mybir
+
+F32 = mybir.dt.float32
+BF16 = mybir.dt.bfloat16
+U16 = mybir.dt.uint16
+ADD = mybir.AluOpType.add
+MAX = mybir.AluOpType.max
+
+P = 128
+C, S, N, H, E = 128, 512, 128, 256, 128
+HB = H // P
+R = math.sqrt(0.5)
+
+FLOPS = 2 * C * H * N + 2 * H * E * N
+
+
+def tile_cohf_kernel(tc, x, dst, w, b, w_mu, b_mu, offs, out):
+    nc = tc.nc
+    with (
+        tc.tile_pool(name="held", bufs=1) as held,
+        tc.psum_pool(name="psum", bufs=1) as psum,
+    ):
+        offsets = held.tile([P, N // 16], U16, name="offsets")
+        nc.sync.dma_start(offsets[:], offs)
+        x_sb = held.tile([C, S], F32, name="x_sb")
+        nc.sync.dma_start(x_sb[:], x)
+        dst_sb = held.tile([C, N], F32, name="dst_sb")
+        nc.scalar.dma_start(dst_sb[:], dst)
+        w_sb = held.tile([C, H], BF16, name="w_sb")
+        nc.scalar.dma_start(w_sb[:], w)
+        w_mu_sb = held.tile([P, HB, E], BF16, name="w_mu_sb")
+        nc.sync.dma_start(w_mu_sb[:], w_mu.rearrange("(k p) e -> p k e", p=P))
+        b_sb = [held.tile([P, 1], F32, name=f"b_sb{k}") for k in range(HB)]
+        for k in range(HB):
+            nc.scalar.dma_start(b_sb[k][:], b[k * P : (k + 1) * P, :])
+        b_mu_sb = held.tile([E, 1], F32, name="b_mu_sb")
+        nc.scalar.dma_start(b_mu_sb[:], b_mu)
+
+        r_dst = held.tile([C, N], F32, name="r_dst")
+        nc.vector.tensor_scalar_mul(r_dst[:], dst_sb[:], R)
+        picked_sum = held.tile([C, N], F32, name="picked_sum")
+        nc.vector.tensor_tensor(picked_sum[:], x_sb[:].indirect(offsets[:]), r_dst[:], ADD)
+        agg = held.tile([C, N], BF16, name="agg")
+        nc.vector.tensor_scalar_mul(agg[:], picked_sum[:], R)
+
+        rep = held.tile([P, HB, N], BF16, name="rep")
+        for k in range(HB):
+            rep_ps = psum.tile([P, N], F32, name=f"rep_ps{k}")
+            nc.tensor.matmul(rep_ps[:], w_sb[:, k * P : (k + 1) * P], agg[:], start=True, stop=True)
+            nc.vector.tensor_scalar(rep[:, k, :], rep_ps[:], b_sb[k][:], 0.0, ADD, MAX)
+
+        out_ps = psum.tile([E, N], F32, name="out_ps")
+        for k in range(HB):
+            nc.tensor.matmul(out_ps[:], w_mu_sb[:, k, :], rep[:, k, :], start=(k == 0), stop=(k == HB - 1))
+        out_sb = held.tile([E, N], F32, name="out_sb")
+        nc.vector.tensor_scalar(out_sb[:], out_ps[:], b_mu_sb[:], 0.0, ADD, MAX)
+        nc.sync.dma_start(out, out_sb[:])

@@ -12,6 +12,7 @@ P = 128
 C, S, N, H, E = 128, 512, 128, 256, 128
 HB = H // P
 R = math.sqrt(0.5)
+X_CUT = (S + N) // 2
 
 FLOPS = 2 * C * H * N + 2 * H * E * N
 
@@ -24,17 +25,18 @@ def tile_cohf_kernel(tc, x, dst, w, b, w_mu, b_mu, offs, out):
     ):
         offsets = held.tile([P, N // 16], U16, name="offsets")
         nc.sync.dma_start(offsets[:], offs)
-        x_sb = held.tile([C, S], F32, name="x_sb")
-        nc.sync.dma_start(x_sb[:], x)
         dst_sb = held.tile([C, N], F32, name="dst_sb")
         nc.scalar.dma_start(dst_sb[:], dst)
+        x_sb = held.tile([C, S], F32, name="x_sb")
+        nc.sync.dma_start(x_sb[:, :X_CUT], x[:, :X_CUT])
+        nc.scalar.dma_start(x_sb[:, X_CUT:], x[:, X_CUT:])
         w_sb = held.tile([C, H], BF16, name="w_sb")
-        nc.scalar.dma_start(w_sb[:], w)
+        nc.sync.dma_start(w_sb[:], w)
         w_mu_sb = held.tile([P, HB, E], BF16, name="w_mu_sb")
-        nc.sync.dma_start(w_mu_sb[:], w_mu.rearrange("(k p) e -> p k e", p=P))
+        nc.scalar.dma_start(w_mu_sb[:], w_mu.rearrange("(k p) e -> p k e", p=P))
         b_sb = [held.tile([P, 1], F32, name=f"b_sb{k}") for k in range(HB)]
         for k in range(HB):
-            nc.scalar.dma_start(b_sb[k][:], b[k * P : (k + 1) * P, :])
+            nc.sync.dma_start(b_sb[k][:], b[k * P : (k + 1) * P, :])
         b_mu_sb = held.tile([E, 1], F32, name="b_mu_sb")
         nc.scalar.dma_start(b_mu_sb[:], b_mu)
 

@@ -12,7 +12,8 @@ P = 128
 C, S, N, H, E = 128, 512, 128, 256, 128
 HB = H // P
 R = math.sqrt(0.5)
-X_CUT = (S + N) // 2
+BANK = 512
+N_WARM = 6
 
 FLOPS = 2 * C * H * N + 2 * H * E * N
 
@@ -23,20 +24,25 @@ def tile_cohf_kernel(tc, x, dst, w, b, w_mu, b_mu, offs, out):
         tc.tile_pool(name="held", bufs=1) as held,
         tc.psum_pool(name="psum", bufs=1) as psum,
     ):
+        zeros = held.tile([P, BANK], BF16, name="zeros")
+        nc.vector.memset(zeros[:], 0.0)
+        warm_ps = psum.tile([P, BANK], F32, name="warm_ps")
+        for i in range(N_WARM):
+            nc.tensor.matmul(warm_ps[:], zeros[:, :P], zeros[:], start=True, stop=True)
+
         offsets = held.tile([P, N // 16], U16, name="offsets")
         nc.sync.dma_start(offsets[:], offs)
+        x_sb = held.tile([C, S], F32, name="x_sb")
+        nc.sync.dma_start(x_sb[:], x)
         dst_sb = held.tile([C, N], F32, name="dst_sb")
         nc.scalar.dma_start(dst_sb[:], dst)
-        x_sb = held.tile([C, S], F32, name="x_sb")
-        nc.sync.dma_start(x_sb[:, :X_CUT], x[:, :X_CUT])
-        nc.scalar.dma_start(x_sb[:, X_CUT:], x[:, X_CUT:])
         w_sb = held.tile([C, H], BF16, name="w_sb")
-        nc.sync.dma_start(w_sb[:], w)
+        nc.scalar.dma_start(w_sb[:], w)
         w_mu_sb = held.tile([P, HB, E], BF16, name="w_mu_sb")
-        nc.scalar.dma_start(w_mu_sb[:], w_mu.rearrange("(k p) e -> p k e", p=P))
+        nc.sync.dma_start(w_mu_sb[:], w_mu.rearrange("(k p) e -> p k e", p=P))
         b_sb = [held.tile([P, 1], F32, name=f"b_sb{k}") for k in range(HB)]
         for k in range(HB):
-            nc.sync.dma_start(b_sb[k][:], b[k * P : (k + 1) * P, :])
+            nc.scalar.dma_start(b_sb[k][:], b[k * P : (k + 1) * P, :])
         b_mu_sb = held.tile([E, 1], F32, name="b_mu_sb")
         nc.scalar.dma_start(b_mu_sb[:], b_mu)
 

@@ -12,8 +12,7 @@ P = 128
 C, S, N, H, E = 128, 512, 128, 256, 128
 HB = H // P
 R = math.sqrt(0.5)
-BANK = 512
-N_WARM = 6
+N_WARM = 18
 
 FLOPS = 2 * C * H * N + 2 * H * E * N
 
@@ -24,11 +23,11 @@ def tile_cohf_kernel(tc, x, dst, w, b, w_mu, b_mu, offs, out):
         tc.tile_pool(name="held", bufs=1) as held,
         tc.psum_pool(name="psum", bufs=1) as psum,
     ):
-        zeros = held.tile([P, BANK], BF16, name="zeros")
+        zeros = held.tile([P, P], BF16, name="zeros")
         nc.vector.memset(zeros[:], 0.0)
-        warm_ps = psum.tile([P, BANK], F32, name="warm_ps")
+        warm_ps = psum.tile([P, P], F32, name="warm_ps")
         for i in range(N_WARM):
-            nc.tensor.matmul(warm_ps[:], zeros[:, :P], zeros[:], start=True, stop=True)
+            nc.tensor.matmul(warm_ps[:], zeros[:], zeros[:], start=True, stop=True)
 
         offsets = held.tile([P, N // 16], U16, name="offsets")
         nc.sync.dma_start(offsets[:], offs)

@@ -12,7 +12,6 @@ P = 128
 C, S, N, H, E = 128, 512, 128, 256, 128
 HB = H // P
 R = math.sqrt(0.5)
-N_WARM = 18
 
 FLOPS = 2 * C * H * N + 2 * H * E * N
 
@@ -23,27 +22,21 @@ def tile_cohf_kernel(tc, x, dst, w, b, w_mu, b_mu, offs, out):
         tc.tile_pool(name="held", bufs=1) as held,
         tc.psum_pool(name="psum", bufs=1) as psum,
     ):
-        zeros = held.tile([P, P], BF16, name="zeros")
-        nc.vector.memset(zeros[:], 0.0)
-        warm_ps = psum.tile([P, P], F32, name="warm_ps")
-        for i in range(N_WARM):
-            nc.tensor.matmul(warm_ps[:], zeros[:], zeros[:], start=True, stop=True)
-
         offsets = held.tile([P, N // 16], U16, name="offsets")
         nc.sync.dma_start(offsets[:], offs)
         x_sb = held.tile([C, S], F32, name="x_sb")
         nc.sync.dma_start(x_sb[:], x)
+        b_sb = [held.tile([P, 1], F32, name=f"b_sb{k}") for k in range(HB)]
+        for k in range(HB):
+            nc.scalar.dma_start(b_sb[k][:], b[k * P : (k + 1) * P, :])
+        b_mu_sb = held.tile([E, 1], F32, name="b_mu_sb")
+        nc.scalar.dma_start(b_mu_sb[:], b_mu)
         dst_sb = held.tile([C, N], F32, name="dst_sb")
         nc.scalar.dma_start(dst_sb[:], dst)
         w_sb = held.tile([C, H], BF16, name="w_sb")
         nc.scalar.dma_start(w_sb[:], w)
         w_mu_sb = held.tile([P, HB, E], BF16, name="w_mu_sb")
         nc.sync.dma_start(w_mu_sb[:], w_mu.rearrange("(k p) e -> p k e", p=P))
-        b_sb = [held.tile([P, 1], F32, name=f"b_sb{k}") for k in range(HB)]
-        for k in range(HB):
-            nc.scalar.dma_start(b_sb[k][:], b[k * P : (k + 1) * P, :])
-        b_mu_sb = held.tile([E, 1], F32, name="b_mu_sb")
-        nc.scalar.dma_start(b_mu_sb[:], b_mu)
 
         r_dst = held.tile([C, N], F32, name="r_dst")
         nc.vector.tensor_scalar_mul(r_dst[:], dst_sb[:], R)

@@ -22,21 +22,21 @@ def tile_cohf_kernel(tc, x, dst, w, b, w_mu, b_mu, offs, out):
         tc.tile_pool(name="held", bufs=1) as held,
         tc.psum_pool(name="psum", bufs=1) as psum,
     ):
+        x_sb = held.tile([C, S], F32, name="x_sb")
+        nc.scalar.dma_start(x_sb[:], x)
         offsets = held.tile([P, N // 16], U16, name="offsets")
         nc.sync.dma_start(offsets[:], offs)
-        x_sb = held.tile([C, S], F32, name="x_sb")
-        nc.sync.dma_start(x_sb[:], x)
+        dst_sb = held.tile([C, N], F32, name="dst_sb")
+        nc.sync.dma_start(dst_sb[:], dst)
+        w_sb = held.tile([C, H], BF16, name="w_sb")
+        nc.scalar.dma_start(w_sb[:], w)
         b_sb = [held.tile([P, 1], F32, name=f"b_sb{k}") for k in range(HB)]
         for k in range(HB):
             nc.scalar.dma_start(b_sb[k][:], b[k * P : (k + 1) * P, :])
-        b_mu_sb = held.tile([E, 1], F32, name="b_mu_sb")
-        nc.scalar.dma_start(b_mu_sb[:], b_mu)
-        dst_sb = held.tile([C, N], F32, name="dst_sb")
-        nc.scalar.dma_start(dst_sb[:], dst)
-        w_sb = held.tile([C, H], BF16, name="w_sb")
-        nc.scalar.dma_start(w_sb[:], w)
         w_mu_sb = held.tile([P, HB, E], BF16, name="w_mu_sb")
         nc.sync.dma_start(w_mu_sb[:], w_mu.rearrange("(k p) e -> p k e", p=P))
+        b_mu_sb = held.tile([E, 1], F32, name="b_mu_sb")
+        nc.sync.dma_start(b_mu_sb[:], b_mu)
 
         r_dst = held.tile([C, N], F32, name="r_dst")
         nc.vector.tensor_scalar_mul(r_dst[:], dst_sb[:], R)

@@ -22,21 +22,21 @@ def tile_cohf_kernel(tc, x, dst, w, b, w_mu, b_mu, offs, out):
         tc.tile_pool(name="held", bufs=1) as held,
         tc.psum_pool(name="psum", bufs=1) as psum,
     ):
-        x_sb = held.tile([C, S], F32, name="x_sb")
-        nc.scalar.dma_start(x_sb[:], x)
         offsets = held.tile([P, N // 16], U16, name="offsets")
         nc.sync.dma_start(offsets[:], offs)
+        x_sb = held.tile([C, S], F32, name="x_sb")
+        nc.sync.dma_start(x_sb[:], x)
         dst_sb = held.tile([C, N], F32, name="dst_sb")
-        nc.sync.dma_start(dst_sb[:], dst)
+        nc.scalar.dma_start(dst_sb[:], dst)
         w_sb = held.tile([C, H], BF16, name="w_sb")
         nc.scalar.dma_start(w_sb[:], w)
-        b_sb = [held.tile([P, 1], F32, name=f"b_sb{k}") for k in range(HB)]
-        for k in range(HB):
-            nc.scalar.dma_start(b_sb[k][:], b[k * P : (k + 1) * P, :])
         w_mu_sb = held.tile([P, HB, E], BF16, name="w_mu_sb")
         nc.sync.dma_start(w_mu_sb[:], w_mu.rearrange("(k p) e -> p k e", p=P))
+        b_sb = held.tile([P, HB], F32, name="b_sb")
+        with nc.allow_non_contiguous_dma(reason="a bias is one number for each partition"):
+            nc.scalar.dma_start(b_sb[:], b.rearrange("(k p) o -> p (k o)", p=P))
         b_mu_sb = held.tile([E, 1], F32, name="b_mu_sb")
-        nc.sync.dma_start(b_mu_sb[:], b_mu)
+        nc.scalar.dma_start(b_mu_sb[:], b_mu)
 
         r_dst = held.tile([C, N], F32, name="r_dst")
         nc.vector.tensor_scalar_mul(r_dst[:], dst_sb[:], R)
@@ -49,7 +49,7 @@ def tile_cohf_kernel(tc, x, dst, w, b, w_mu, b_mu, offs, out):
         for k in range(HB):
             rep_ps = psum.tile([P, N], F32, name=f"rep_ps{k}")
             nc.tensor.matmul(rep_ps[:], w_sb[:, k * P : (k + 1) * P], agg[:], start=True, stop=True)
-            nc.vector.tensor_scalar(rep[:, k, :], rep_ps[:], b_sb[k][:], 0.0, ADD, MAX)
+            nc.vector.tensor_scalar(rep[:, k, :], rep_ps[:], b_sb[:, k : k + 1], 0.0, ADD, MAX)
 
         out_ps = psum.tile([E, N], F32, name="out_ps")
         for k in range(HB):

@@ -12,6 +12,8 @@ P = 128
 C, S, N, H, E = 128, 512, 128, 256, 128
 HB = H // P
 R = math.sqrt(0.5)
+BANK = 512
+N_WARM = 6
 
 FLOPS = 2 * C * H * N + 2 * H * E * N
 
@@ -22,6 +24,12 @@ def tile_cohf_kernel(tc, x, dst, w, b, w_mu, b_mu, offs, out):
         tc.tile_pool(name="held", bufs=1) as held,
         tc.psum_pool(name="psum", bufs=1) as psum,
     ):
+        zeros = held.tile([P, BANK], BF16, name="zeros")
+        nc.vector.memset(zeros[:], 0.0)
+        warm_ps = psum.tile([P, BANK], F32, name="warm_ps")
+        for i in range(N_WARM):
+            nc.tensor.matmul(warm_ps[:], zeros[:, :P], zeros[:], start=True, stop=True)
+
         offsets = held.tile([P, N // 16], U16, name="offsets")
         nc.sync.dma_start(offsets[:], offs)
         x_sb = held.tile([C, S], F32, name="x_sb")

@@ -14,6 +14,8 @@ HB = H // P
 R = math.sqrt(0.5)
 BANK = 512
 N_WARM = 6
+PIECES = 2
+NP = N // PIECES
 
 FLOPS = 2 * C * H * N + 2 * H * E * N
 
@@ -46,22 +48,32 @@ def tile_cohf_kernel(tc, x, dst, w, b, w_mu, b_mu, offs, out):
         b_mu_sb = held.tile([E, 1], F32, name="b_mu_sb")
         nc.scalar.dma_start(b_mu_sb[:], b_mu)
 
+        cols = [slice(i * NP, (i + 1) * NP) for i in range(PIECES)]
+
         r_dst = held.tile([C, N], F32, name="r_dst")
         nc.vector.tensor_scalar_mul(r_dst[:], dst_sb[:], R)
         picked_sum = held.tile([C, N], F32, name="picked_sum")
-        nc.vector.tensor_tensor(picked_sum[:], x_sb[:].indirect(offsets[:]), r_dst[:], ADD)
+        for i in range(PIECES):
+            piece_offsets = offsets[:, i * (NP // 16) : (i + 1) * (NP // 16)]
+            nc.vector.tensor_tensor(picked_sum[:, cols[i]], x_sb[:].indirect(piece_offsets), r_dst[:, cols[i]], ADD)
         agg = held.tile([C, N], BF16, name="agg")
-        nc.vector.tensor_scalar_mul(agg[:], picked_sum[:], R)
+        for i in range(PIECES):
+            nc.vector.tensor_scalar_mul(agg[:, cols[i]], picked_sum[:, cols[i]], R)
 
+        rep_ps = [[psum.tile([P, NP], F32, name=f"rep_ps{i}{k}") for k in range(HB)] for i in range(PIECES)]
+        for i in range(PIECES):
+            for k in range(HB):
+                nc.tensor.matmul(rep_ps[i][k][:], w_sb[:, k * P : (k + 1) * P], agg[:, cols[i]], start=True, stop=True)
         rep = held.tile([P, HB, N], BF16, name="rep")
-        for k in range(HB):
-            rep_ps = psum.tile([P, N], F32, name=f"rep_ps{k}")
-            nc.tensor.matmul(rep_ps[:], w_sb[:, k * P : (k + 1) * P], agg[:], start=True, stop=True)
-            nc.vector.tensor_scalar(rep[:, k, :], rep_ps[:], b_sb[:, k : k + 1], 0.0, ADD, MAX)
+        for i in range(PIECES):
+            for k in range(HB):
+                nc.vector.tensor_scalar(rep[:, k, cols[i]], rep_ps[i][k][:], b_sb[:, k : k + 1], 0.0, ADD, MAX)
 
-        out_ps = psum.tile([E, N], F32, name="out_ps")
-        for k in range(HB):
-            nc.tensor.matmul(out_ps[:], w_mu_sb[:, k, :], rep[:, k, :], start=(k == 0), stop=(k == HB - 1))
+        out_ps = [psum.tile([E, NP], F32, name=f"out_ps{i}") for i in range(PIECES)]
+        for i in range(PIECES):
+            for k in range(HB):
+                nc.tensor.matmul(out_ps[i][:], w_mu_sb[:, k, :], rep[:, k, cols[i]], start=(k == 0), stop=(k == HB - 1))
         out_sb = held.tile([E, N], F32, name="out_sb")
-        nc.vector.tensor_scalar(out_sb[:], out_ps[:], b_mu_sb[:], 0.0, ADD, MAX)
+        for i in range(PIECES):
+            nc.vector.tensor_scalar(out_sb[:, cols[i]], out_ps[i][:], b_mu_sb[:], 0.0, ADD, MAX)
         nc.sync.dma_start(out, out_sb[:])

@@ -12,8 +12,6 @@ P = 128
 C, S, N, H, E = 128, 512, 128, 256, 128
 HB = H // P
 R = math.sqrt(0.5)
-BANK = 512
-N_WARM = 6
 PIECES = 2
 NP = N // PIECES
 
@@ -26,12 +24,6 @@ def tile_cohf_kernel(tc, x, dst, w, b, w_mu, b_mu, offs, out):
         tc.tile_pool(name="held", bufs=1) as held,
         tc.psum_pool(name="psum", bufs=1) as psum,
     ):
-        zeros = held.tile([P, BANK], BF16, name="zeros")
-        nc.vector.memset(zeros[:], 0.0)
-        warm_ps = psum.tile([P, BANK], F32, name="warm_ps")
-        for i in range(N_WARM):
-            nc.tensor.matmul(warm_ps[:], zeros[:, :P], zeros[:], start=True, stop=True)
-
         offsets = held.tile([P, N // 16], U16, name="offsets")
         nc.sync.dma_start(offsets[:], offs)
         x_sb = held.tile([C, S], F32, name="x_sb")

@@ -33,10 +33,9 @@ def tile_cohf_kernel(tc, x, dst, w, b, w_mu, b_mu, offs, out):
         w_sb = held.tile([C, H], BF16, name="w_sb")
         nc.scalar.dma_start(w_sb[:], w)
         w_mu_sb = held.tile([P, HB, E], BF16, name="w_mu_sb")
-        nc.sync.dma_start(w_mu_sb[:], w_mu.rearrange("(k p) e -> p k e", p=P))
+        nc.sync.dma_start(w_mu_sb[:], w_mu.rearrange("(p k) e -> p k e", k=HB))
         b_sb = held.tile([P, HB], F32, name="b_sb")
-        with nc.allow_non_contiguous_dma(reason="a bias is one number for each partition"):
-            nc.scalar.dma_start(b_sb[:], b.rearrange("(k p) o -> p (k o)", p=P))
+        nc.scalar.dma_start(b_sb[:], b.rearrange("(p k) o -> p (k o)", k=HB))
         b_mu_sb = held.tile([E, 1], F32, name="b_mu_sb")
         nc.scalar.dma_start(b_mu_sb[:], b_mu)
 
@@ -55,7 +54,7 @@ def tile_cohf_kernel(tc, x, dst, w, b, w_mu, b_mu, offs, out):
         rep_ps = [[psum.tile([P, NP], F32, name=f"rep_ps{i}{k}") for k in range(HB)] for i in range(PIECES)]
         for i in range(PIECES):
             for k in range(HB):
-                nc.tensor.matmul(rep_ps[i][k][:], w_sb[:, k * P : (k + 1) * P], agg[:, cols[i]], start=True, stop=True)
+                nc.tensor.matmul(rep_ps[i][k][:], w_sb[:, k::HB], agg[:, cols[i]], start=True, stop=True)
         rep = held.tile([P, HB, N], BF16, name="rep")
         for i in range(PIECES):
             for k in range(HB):

@@ -7,6 +7,7 @@ BF16 = mybir.dt.bfloat16
 U16 = mybir.dt.uint16
 ADD = mybir.AluOpType.add
 MAX = mybir.AluOpType.max
+RELU = mybir.ActivationFunctionType.Relu
 
 P = 128
 C, S, N, H, E = 128, 512, 128, 256, 128
@@ -39,6 +40,11 @@ def tile_cohf_kernel(tc, x, dst, w, b, w_mu, b_mu, offs, out):
         b_mu_sb = held.tile([E, 1], F32, name="b_mu_sb")
         nc.scalar.dma_start(b_mu_sb[:], b_mu)
 
+        zeros = held.tile([P, 1], F32, name="zeros")
+        nc.vector.memset(zeros[:], 0.0)
+        early = held.tile([P, 1], F32, name="early")
+        nc.scalar.activation(early[:], zeros[:], RELU)
+
         cols = [slice(i * NP, (i + 1) * NP) for i in range(PIECES)]
 
         r_dst = held.tile([C, N], F32, name="r_dst")
@@ -57,8 +63,8 @@ def tile_cohf_kernel(tc, x, dst, w, b, w_mu, b_mu, offs, out):
                 nc.tensor.matmul(rep_ps[i][k][:], w_sb[:, k::HB], agg[:, cols[i]], start=True, stop=True)
         rep = held.tile([P, HB, N], BF16, name="rep")
         for i in range(PIECES):
-            for k in range(HB):
-                nc.vector.tensor_scalar(rep[:, k, cols[i]], rep_ps[i][k][:], b_sb[:, k : k + 1], 0.0, ADD, MAX)
+            nc.vector.tensor_scalar(rep[:, 0, cols[i]], rep_ps[i][0][:], b_sb[:, 0:1], 0.0, ADD, MAX)
+            nc.scalar.activation(rep[:, 1, cols[i]], rep_ps[i][1][:], RELU, bias=b_sb[:, 1:2])
 
         out_ps = [psum.tile([E, NP], F32, name=f"out_ps{i}") for i in range(PIECES)]
         for i in range(PIECES):

@@ -63,8 +63,8 @@ def tile_cohf_kernel(tc, x, dst, w, b, w_mu, b_mu, offs, out):
                 nc.tensor.matmul(rep_ps[i][k][:], w_sb[:, k::HB], agg[:, cols[i]], start=True, stop=True)
         rep = held.tile([P, HB, N], BF16, name="rep")
         for i in range(PIECES):
-            nc.vector.tensor_scalar(rep[:, 0, cols[i]], rep_ps[i][0][:], b_sb[:, 0:1], 0.0, ADD, MAX)
-            nc.scalar.activation(rep[:, 1, cols[i]], rep_ps[i][1][:], RELU, bias=b_sb[:, 1:2])
+            nc.scalar.activation(rep[:, 0, cols[i]], rep_ps[i][0][:], RELU, bias=b_sb[:, 0:1])
+            nc.vector.tensor_scalar(rep[:, 1, cols[i]], rep_ps[i][1][:], b_sb[:, 1:2], 0.0, ADD, MAX)
 
         out_ps = [psum.tile([E, NP], F32, name=f"out_ps{i}") for i in range(PIECES)]
         for i in range(PIECES):

import math

import concourse.mybir as mybir

F32 = mybir.dt.float32
BF16 = mybir.dt.bfloat16
U16 = mybir.dt.uint16
ADD = mybir.AluOpType.add
MAX = mybir.AluOpType.max
RELU = mybir.ActivationFunctionType.Relu

P = 128
C, S, N, H, E = 128, 512, 128, 256, 128
HB = H // P
R = math.sqrt(0.5)
PIECES = 2
NP = N // PIECES

FLOPS = 2 * C * H * N + 2 * H * E * N


def tile_cohf_kernel(tc, x, dst, w, b, w_mu, b_mu, offs, out):
    nc = tc.nc
    with (
        tc.tile_pool(name="held", bufs=1) as held,
        tc.psum_pool(name="psum", bufs=1) as psum,
    ):
        offsets = held.tile([P, N // 16], U16, name="offsets")
        nc.sync.dma_start(offsets[:], offs)
        x_sb = held.tile([C, S], F32, name="x_sb")
        nc.sync.dma_start(x_sb[:], x)
        dst_sb = held.tile([C, N], F32, name="dst_sb")
        nc.scalar.dma_start(dst_sb[:], dst)
        w_sb = held.tile([C, H], BF16, name="w_sb")
        nc.scalar.dma_start(w_sb[:], w)
        w_mu_sb = held.tile([P, HB, E], BF16, name="w_mu_sb")
        nc.sync.dma_start(w_mu_sb[:], w_mu.rearrange("(p k) e -> p k e", k=HB))
        b_sb = held.tile([P, HB], F32, name="b_sb")
        nc.scalar.dma_start(b_sb[:], b.rearrange("(p k) o -> p (k o)", k=HB))
        b_mu_sb = held.tile([E, 1], F32, name="b_mu_sb")
        nc.scalar.dma_start(b_mu_sb[:], b_mu)

        zeros = held.tile([P, 1], F32, name="zeros")
        nc.vector.memset(zeros[:], 0.0)
        early = held.tile([P, 1], F32, name="early")
        nc.scalar.activation(early[:], zeros[:], RELU)

        cols = [slice(i * NP, (i + 1) * NP) for i in range(PIECES)]

        r_dst = held.tile([C, N], F32, name="r_dst")
        nc.vector.tensor_scalar_mul(r_dst[:], dst_sb[:], R)
        picked_sum = held.tile([C, N], F32, name="picked_sum")
        for i in range(PIECES):
            piece_offsets = offsets[:, i * (NP // 16) : (i + 1) * (NP // 16)]
            nc.vector.tensor_tensor(picked_sum[:, cols[i]], x_sb[:].indirect(piece_offsets), r_dst[:, cols[i]], ADD)
        agg = held.tile([C, N], BF16, name="agg")
        for i in range(PIECES):
            nc.vector.tensor_scalar_mul(agg[:, cols[i]], picked_sum[:, cols[i]], R)

        rep_ps = [[psum.tile([P, NP], F32, name=f"rep_ps{i}{k}") for k in range(HB)] for i in range(PIECES)]
        for i in range(PIECES):
            for k in range(HB):
                nc.tensor.matmul(rep_ps[i][k][:], w_sb[:, k::HB], agg[:, cols[i]], start=True, stop=True)
        rep = held.tile([P, HB, N], BF16, name="rep")
        for i in range(PIECES):
            nc.scalar.activation(rep[:, 0, cols[i]], rep_ps[i][0][:], RELU, bias=b_sb[:, 0:1])
            nc.vector.tensor_scalar(rep[:, 1, cols[i]], rep_ps[i][1][:], b_sb[:, 1:2], 0.0, ADD, MAX)

        out_ps = [psum.tile([E, NP], F32, name=f"out_ps{i}") for i in range(PIECES)]
        for i in range(PIECES):
            for k in range(HB):
                nc.tensor.matmul(out_ps[i][:], w_mu_sb[:, k, :], rep[:, k, cols[i]], start=(k == 0), stop=(k == HB - 1))
        out_sb = held.tile([E, N], F32, name="out_sb")
        for i in range(PIECES):
            nc.vector.tensor_scalar(out_sb[:, cols[i]], out_ps[i][:], b_mu_sb[:], 0.0, ADD, MAX)
        nc.sync.dma_start(out, out_sb[:])
